import numpy as np
import ml_dtypes


def mxq(x, axis, fmt="e4m3"):
    dtype, down = {"e4m3": (ml_dtypes.float8_e4m3fn, 7), "e5m2": (ml_dtypes.float8_e5m2, 14)}[fmt]
    v = np.moveaxis(np.asarray(x, np.float32).astype(ml_dtypes.bfloat16).astype(np.float64), axis, -1)
    blocks = v.reshape(v.shape[:-1] + (-1, 32))
    amax = np.abs(blocks).max(-1, keepdims=True)
    byte = np.maximum(np.where(amax > 0, np.frexp(amax)[1] - 1 + 127, 0) - down, 1)
    scale = np.exp2(byte - 127.0)
    codes = (blocks / scale).astype(np.float32).astype(dtype).astype(np.float64)
    return np.moveaxis((codes * scale).reshape(v.shape), -1, axis)


WIDE = False


def mx_kscale(k):
    if not WIDE:
        return np.ones(k)
    levels = np.array([10, -10, 5, -5, 0])
    a = np.random.permutation(np.resize(levels, k // 512 * 4)).reshape(k // 512, 4)
    idx = np.arange(k)
    return np.exp2(a[idx // 512, idx % 128 // 32])


BF16 = ml_dtypes.bfloat16


def bf(x):
    return np.asarray(x, np.float32).astype(BF16)


def f64(x):
    return np.asarray(x).astype(np.float64)


B, N, H, D, C, O = 2048, 3, 1024, 256, 512, 256
F = D + D + C


def setup_inputs():
    s = mx_kscale(F)
    t = mx_kscale(H)
    ri, rt = mx_kscale(H), mx_kscale(H)
    return {
        "input_text": bf(np.random.standard_normal((B, D)) * s[:D])[:, None, :],
        "input_img": bf(np.random.standard_normal((B, D)) * s[D:D + D])[:, None, :],
        "input_compress": bf(np.random.standard_normal((B, C)) * s[D + D:]),
        "base_text_features": bf(np.random.standard_normal((B, N, H)) * rt),
        "base_img_features": bf(np.random.standard_normal((B, N, H)) * ri),
        "W_user": bf(np.random.standard_normal((H, F)) / np.sqrt(F) / s * t[:, None]),
        "b_user": bf(np.random.standard_normal(H) * 0.3 * t),
        "Wl_img": bf(np.random.standard_normal((O, H)) * 0.5 * np.sqrt(N / H) / ri),
        "bl_img": bf(np.random.standard_normal(O) * 0.2),
        "Wr_img": bf(np.random.standard_normal((O, H)) * 0.5 / np.sqrt(H) / t),
        "Wl_txt": bf(np.random.standard_normal((O, H)) * 0.5 * np.sqrt(N / H) / rt),
        "bl_txt": bf(np.random.standard_normal(O) * 0.2),
        "Wr_txt": bf(np.random.standard_normal((O, H)) * 0.5 / np.sqrt(H) / t),
    }


def reference(input_text, input_img, input_compress, base_text_features, base_img_features,
              W_user, b_user, Wl_img, bl_img, Wr_img, Wl_txt, bl_txt, Wr_txt):
    feat = np.concatenate([f64(input_text)[:, 0], f64(input_img)[:, 0], f64(input_compress)], axis=-1)
    u = (mxq(feat, 1, "e4m3") @ mxq(f64(W_user), 1, "e4m3").T) + f64(b_user)
    mean_img = f64(base_img_features).mean(axis=1)
    mean_txt = f64(base_text_features).mean(axis=1)
    uq = mxq(u, 1, "e4m3")
    out = ((mxq(mean_img, 1, "e4m3") @ mxq(f64(Wl_img), 1, "e4m3").T) + f64(bl_img)
           + (uq @ mxq(f64(Wr_img), 1, "e4m3").T)
           + (mxq(mean_txt, 1, "e4m3") @ mxq(f64(Wl_txt), 1, "e4m3").T) + f64(bl_txt)
           + (uq @ mxq(f64(Wr_txt), 1, "e4m3").T))
    return np.maximum(out, 0.0)

@@ -1,0 +1,335 @@
+from contextlib import ExitStack
+
+import concourse.mybir as mybir
+from concourse.masks import make_identity
+
+F32 = mybir.dt.float32
+BF16 = mybir.dt.bfloat16
+U32 = mybir.dt.uint32
+U8 = mybir.dt.uint8
+FP8X4 = mybir.dt.float8_e4m3fn_x4
+ACT = mybir.ActivationFunctionType
+ADD = mybir.AluOpType.add
+
+P = 128
+USERS, NODES, H, O = 2048, 3, 1024, 256
+TILES = USERS // P
+ROUNDS = TILES // 2
+PASSES = H // (4 * P)
+CHUNKS = H // P
+BASE_BUFS = 4
+FLOPS = 2 * USERS * H * H + 4 * 2 * USERS * H * O
+
+
+def tile_graphlearner_ib_pa_t_kernel(
+    tc,
+    input_text,
+    input_img,
+    input_compress,
+    base_text_features,
+    base_img_features,
+    W_user,
+    b_user,
+    Wl_img,
+    bl_img,
+    Wr_img,
+    Wl_txt,
+    bl_txt,
+    Wr_txt,
+    out,
+):
+    nc = tc.nc
+    text_v = input_text.rearrange("(p t) o d -> p t (o d)", t=TILES)
+    imgf_v = input_img.rearrange("(p t) o d -> p t (o d)", t=TILES)
+    comp_v = input_compress.rearrange("(p t) d -> p t d", t=TILES)
+    base_v = (
+        base_img_features.rearrange("(p t) n h -> p t n h", t=TILES),
+        base_text_features.rearrange("(p t) n h -> p t n h", t=TILES),
+    )
+    out_v = out.rearrange("(p t) o -> p t o", t=TILES)
+
+    with ExitStack() as stack:
+        keep = stack.enter_context(tc.tile_pool(name="keep", bufs=1))
+        base_pool = stack.enter_context(tc.tile_pool(name="base", bufs=BASE_BUFS))
+        work = stack.enter_context(tc.tile_pool(name="work", bufs=2))
+        codes_pool = stack.enter_context(tc.tile_pool(name="codes", bufs=4))
+        tp_pool = stack.enter_context(tc.psum_pool(name="tp", bufs=4))
+        u_pool = stack.enter_context(tc.psum_pool(name="ups", bufs=3))
+        o_pool = stack.enter_context(tc.psum_pool(name="ops", bufs=1))
+        stack.enter_context(tc.manual_schedule())
+
+        ident = keep.tile([P, P], F32, name="ident")
+        make_identity(nc, ident[:])
+
+        bu_bf = keep.tile([P, 4, 2], BF16, name="bu_bf")
+        nc.scalar.dma_start(out=bu_bf[:], in_=b_user.rearrange("(c p e) -> p c e", c=4, p=P, e=2))
+        bl_a = keep.tile([P, O], BF16, name="bl_a")
+        nc.scalar.dma_start(out=bl_a[:], in_=bl_img.partition_broadcast(P))
+        bl_b = keep.tile([P, O], BF16, name="bl_b")
+        nc.scalar.dma_start(out=bl_b[:], in_=bl_txt.partition_broadcast(P))
+        bu = keep.tile([P, CHUNKS], F32, name="bu")
+        bl2 = keep.tile([P, 2, O], F32, name="bl2")
+
+        wu_raw = keep.tile([P, 4, 2, H], BF16, name="wu_raw")
+        ws_raw = keep.tile([P, 4, 2, H], BF16, name="ws_raw")
+        wu_codes = keep.tile([P, CHUNKS, PASSES, P], U32, name="wu_codes", align_bytes=64)
+        wu_scales = keep.tile([P, CHUNKS, PASSES, P], U8, name="wu_scales", align_bytes=64)
+        ws_codes = keep.tile([P, 4, PASSES, O], U32, name="ws_codes", align_bytes=64)
+        ws_scales = keep.tile([P, 4, PASSES, O], U8, name="ws_scales", align_bytes=64)
+
+        nodes, feats, sums, grouped, mean_q, feat_q, planes, u_q, acc = {}, {}, {}, {}, {}, {}, {}, {}, {}
+
+        def words_out(bank):
+            return bank[:].rearrange("p (g u) r -> p g r u", u=2)
+
+        def words_in(ap):
+            return ap.bitcast(F32).rearrange("p g (r u) -> p g r u", u=2)
+
+        def transpose_words(rows):
+            bank = tp_pool.tile([P, 4, P], F32, name="bank", tag="bank")
+            for k in range(4):
+                nc.tensor.transpose(out=bank[:, k, :], in_=rows[k], identity=ident[:])
+            return bank
+
+        def quantise(values, codes, scales):
+            nc.vector.quantize_mx(out=codes.bitcast(FP8X4), scales=scales, in_=values)
+
+        def load_base(s):
+            for x in range(2):
+                t = base_pool.tile([P, NODES, H], BF16, name="nodes%d" % x, tag="nodes%d" % x)
+                nc.sync.dma_start(out=t[:], in_=base_v[x][:, s])
+                nodes[(s, x)] = t
+
+        def load_feat(q):
+            cols = slice(4 * q, 4 * q + 4)
+            text = work.tile([P, 4, 256], BF16, name="text", tag="text")
+            nc.sync.dma_start(out=text[:], in_=text_v[:, cols, :])
+            imgf = work.tile([P, 4, 256], BF16, name="imgf", tag="imgf")
+            nc.sync.dma_start(out=imgf[:], in_=imgf_v[:, cols, :])
+            comp = work.tile([P, 4, 512], BF16, name="comp", tag="comp")
+            nc.sync.dma_start(out=comp[:], in_=comp_v[:, cols, :])
+            feats[q] = (text, imgf, comp)
+
+        def add_nodes(s):
+            def sorted_cols(ap):
+                return ap.rearrange("p (c q e) -> p c e q", c=4, q=P, e=2)
+
+            for x in range(2):
+                total = work.tile([P, 4, 2, P], F32, name="total%d" % x, tag="total%d" % x)
+                sums[(s, x)] = total
+                n = nodes[(s, x)]
+                nc.vector.tensor_tensor(out=total[:], in0=sorted_cols(n[:, 0, :]), in1=sorted_cols(n[:, 1, :]), op=ADD)
+            for x in range(2):
+                total = sums[(s, x)]
+                n = nodes[(s, x)]
+                nc.vector.tensor_tensor(out=total[:], in0=total[:], in1=sorted_cols(n[:, 2, :]), op=ADD)
+
+        def transpose_means(s):
+            mg = work.tile([P, 2, PASSES, P, 4], BF16, name="mg", tag="mg", align_bytes=64)
+            grouped[s] = mg
+            for x in range(2):
+                total = sums[(s, x)]
+                for g in range(PASSES):
+                    bank = tp_pool.tile([P, 4, P], F32, name="bank", tag="bank")
+                    for u in range(2):
+                        for e in range(2):
+                            nc.tensor.transpose(out=bank[:, 2 * u + e, :], in_=total[:, 2 * g + u, e, :], identity=ident[:])
+                    nc.scalar.activation(
+                        out=mg[:, x, g, :, :], in_=bank[:].rearrange("p t r -> p r t"), func=ACT.Copy, scale=1.0 / NODES
+                    )
+
+        def quantise_means(s):
+            codes = codes_pool.tile([P, 2, PASSES, P], U32, name="m_codes", tag="m_codes", align_bytes=64)
+            scales = codes_pool.tile([P, 2, PASSES, P], U8, name="m_scales", tag="m_scales", align_bytes=64)
+            mean_q[s] = (codes, scales)
+            quantise(
+                grouped[s][:].rearrange("p x g r t -> p (x g r t)"),
+                codes[:].rearrange("p x g r -> p (x g r)"),
+                scales[:].rearrange("p x g r -> p (x g r)"),
+            )
+
+        def transpose_feat(rho):
+            fg = work.tile([P, PASSES, 2, 4 * P], BF16, name="fg", tag="fg", align_bytes=64)
+            grouped[("f", rho)] = fg
+            for ti in range(2):
+                q, i = divmod(2 * rho + ti, 4)
+                text, imgf, comp = feats[q]
+                bank = transpose_words(
+                    [
+                        text[:, i, :].bitcast(F32),
+                        imgf[:, i, :].bitcast(F32),
+                        comp[:, i, 0:256].bitcast(F32),
+                        comp[:, i, 256:512].bitcast(F32),
+                    ]
+                )
+                nc.scalar.copy(out=words_in(fg[:, :, ti, :]), in_=words_out(bank))
+
+        def quantise_feat(rho):
+            codes = work.tile([P, PASSES, 2 * P], U32, name="f_codes", tag="f_codes", align_bytes=64)
+            scales = work.tile([P, PASSES, 2 * P], U8, name="f_scales", tag="f_scales", align_bytes=64)
+            feat_q[rho] = (codes, scales)
+            quantise(
+                grouped[("f", rho)][:].rearrange("p g t w -> p (g t w)"),
+                codes[:].rearrange("p g n -> p (g n)"),
+                scales[:].rearrange("p g n -> p (g n)"),
+            )
+
+        def transpose_w_user():
+            wg = keep.tile([P, CHUNKS, PASSES, 4 * P], BF16, name="wg", tag="wgroup", align_bytes=64)
+            grouped["wu"] = wg
+            for j in range(CHUNKS):
+                c, e = divmod(j, 2)
+                words = wu_raw[:, c, e, :].bitcast(F32)
+                bank = transpose_words([words[:, P * k : P * (k + 1)] for k in range(4)])
+                nc.scalar.copy(out=words_in(wg[:, j, :, :]), in_=words_out(bank))
+
+        def quantise_w_user():
+            wg = grouped["wu"]
+            for half in range(2):
+                js = slice(4 * half, 4 * half + 4)
+                quantise(
+                    wg[:, js].rearrange("p j g w -> p (j g w)"),
+                    wu_codes[:, js].rearrange("p j g r -> p (j g r)"),
+                    wu_scales[:, js].rearrange("p j g r -> p (j g r)"),
+                )
+
+        def transpose_w_out():
+            sg = keep.tile([P, 4, PASSES, 2, 4 * P], BF16, name="sg", tag="wgroup", align_bytes=64)
+            grouped["ws"] = sg
+            for m in range(4):
+                for a in range(2):
+                    words = ws_raw[:, m, a, :].bitcast(F32)
+                    bank = transpose_words([words[:, P * k : P * (k + 1)] for k in range(4)])
+                    nc.scalar.copy(out=words_in(sg[:, m, :, a, :]), in_=words_out(bank))
+
+        def quantise_w_out():
+            sg = grouped["ws"]
+            for half in range(2):
+                ms = slice(2 * half, 2 * half + 2)
+                quantise(
+                    sg[:, ms].rearrange("p m g a w -> p (m g a w)"),
+                    ws_codes[:, ms].rearrange("p m g o -> p (m g o)"),
+                    ws_scales[:, ms].rearrange("p m g o -> p (m g o)"),
+                )
+
+        def stage1(rho):
+            codes, scales = feat_q[rho]
+            up = work.tile([P, CHUNKS, 2 * P], BF16, name="up", tag="up")
+            planes[rho] = up
+            for b in range(CHUNKS // 2):
+                ub = u_pool.tile([P, 2, 2 * P], F32, name="ub", tag="ub")
+                for jj in range(2):
+                    j = 2 * b + jj
+                    for g in range(PASSES):
+                        nc.tensor.matmul_mx(
+                            out=ub[:, jj, :],
+                            lhsT=wu_codes[:, j, g, :].bitcast(FP8X4),
+                            lhsT_scale=wu_scales[:, j, g, :],
+                            rhs=codes[:, g, :].bitcast(FP8X4),
+                            rhs_scale=scales[:, g, :],
+                            start=(g == 0),
+                            stop=(g == PASSES - 1),
+                        )
+                for jj in range(2):
+                    j = 2 * b + jj
+                    nc.scalar.activation(out=up[:, j, :], in_=ub[:, jj, :], func=ACT.Identity, bias=bu[:, j : j + 1])
+
+        def regroup_u(rho):
+            ug = work.tile([P, PASSES, 2 * P, 4], BF16, name="ug", tag="ug", align_bytes=64)
+            grouped[("u", rho)] = ug
+            for g in range(PASSES):
+                nc.vector.tensor_copy(
+                    out=ug[:, g, :, :].rearrange("p (c i) t -> p c t i", i=4),
+                    in_=planes[rho][:, 4 * g : 4 * g + 4, :].rearrange("p t (c i) -> p c t i", i=4),
+                )
+
+        def quantise_u(rho):
+            codes = work.tile([P, PASSES, 2 * P], U32, name="u_codes", tag="u_codes", align_bytes=64)
+            scales = work.tile([P, PASSES, 2 * P], U8, name="u_scales", tag="u_scales", align_bytes=64)
+            u_q[rho] = (codes, scales)
+            quantise(
+                grouped[("u", rho)][:].rearrange("p g n t -> p (g n t)"),
+                codes[:].rearrange("p g n -> p (g n)"),
+                scales[:].rearrange("p g n -> p (g n)"),
+            )
+
+        def stage2(rho):
+            ob = o_pool.tile([P, 2, O], F32, name="ob", tag="ob")
+            acc[rho] = ob
+            u_codes, u_scales = u_q[rho]
+            for ti in range(2):
+                m_codes, m_scales = mean_q[2 * rho + ti]
+                cols = slice(P * ti, P * (ti + 1))
+                left = []
+                for g in range(PASSES):
+                    left.append((m_codes[:, 0, g, :], m_scales[:, 0, g, :], 0, g))
+                    left.append((u_codes[:, g, cols], u_scales[:, g, cols], 1, g))
+                    left.append((m_codes[:, 1, g, :], m_scales[:, 1, g, :], 2, g))
+                    left.append((u_codes[:, g, cols], u_scales[:, g, cols], 3, g))
+                for i, (codes, scales, m, g) in enumerate(left):
+                    nc.tensor.matmul_mx(
+                        out=ob[:, ti, :],
+                        lhsT=codes.bitcast(FP8X4),
+                        lhsT_scale=scales,
+                        rhs=ws_codes[:, m, g, :].bitcast(FP8X4),
+                        rhs_scale=ws_scales[:, m, g, :],
+                        start=(i == 0),
+                        stop=(i == len(left) - 1),
+                    )
+
+        def finish(rho):
+            res = work.tile([P, 2, O], F32, name="res", tag="res")
+            nc.vector.tensor_tensor(out=res[:], in0=acc[rho][:], in1=bl2[:], op=ADD)
+            nc.scalar.activation(out=res[:], in_=res[:], func=ACT.Relu)
+            nc.scalar.dma_start(out=out_v[:, 2 * rho : 2 * rho + 2, :], in_=res[:])
+
+        load_base(0)
+        load_feat(0)
+        nc.sync.dma_start(out=wu_raw[:], in_=W_user.rearrange("(c p e) f -> p c e f", c=4, p=P, e=2))
+        load_base(1)
+        load_base(2)
+        for m, w in enumerate((Wl_img, Wr_img, Wl_txt, Wr_txt)):
+            nc.sync.dma_start(out=ws_raw[:, m], in_=w.rearrange("(a p) h -> p a h", a=2))
+        load_base(3)
+
+        for s in range(TILES + 3):
+            rho, odd = divmod(s, 2)
+            if s < TILES:
+                add_nodes(s)
+            if s + BASE_BUFS < TILES:
+                load_base(s + BASE_BUFS)
+            if s % 4 == 1 and (s + 3) // 4 < TILES // 4:
+                load_feat((s + 3) // 4)
+            if s == 0:
+                nc.vector.tensor_copy(out=bu[:], in_=bu_bf[:].rearrange("p c e -> p (c e)"))
+                for ti in range(2):
+                    nc.vector.tensor_tensor(out=bl2[:, ti, :], in0=bl_a[:], in1=bl_b[:], op=ADD)
+            if 1 <= s <= TILES:
+                transpose_means(s - 1)
+            if not odd:
+                if rho < ROUNDS:
+                    transpose_feat(rho)
+                if s == 0:
+                    transpose_w_user()
+                if s == 2:
+                    transpose_w_out()
+            else:
+                if rho < ROUNDS:
+                    stage1(rho)
+                if 1 <= rho <= ROUNDS:
+                    stage2(rho - 1)
+            if not odd and 1 <= rho <= ROUNDS:
+                regroup_u(rho - 1)
+            if 1 <= s <= TILES:
+                quantise_means(s - 1)
+            if not odd:
+                if s == 0:
+                    quantise_w_user()
+                if 1 <= rho <= ROUNDS:
+                    quantise_u(rho - 1)
+                if rho < ROUNDS:
+                    quantise_feat(rho)
+                if s == 2:
+                    quantise_w_out()
+                if 2 <= rho <= ROUNDS + 1:
+                    finish(rho - 2)

@@ -18,6 +18,7 @@ ROUNDS = TILES // 2
 PASSES = H // (4 * P)
 CHUNKS = H // P
 BASE_BUFS = 4
+PE_QUARTERS = 3
 FLOPS = 2 * USERS * H * H + 4 * 2 * USERS * H * O
 
 
@@ -60,6 +61,8 @@ def tile_graphlearner_ib_pa_t_kernel(
 
         ident = keep.tile([P, P], F32, name="ident")
         make_identity(nc, ident[:])
+        ident_bf = keep.tile([P, P], BF16, name="ident_bf")
+        make_identity(nc, ident_bf[:])
 
         bu_bf = keep.tile([P, 4, 2], BF16, name="bu_bf")
         nc.scalar.dma_start(out=bu_bf[:], in_=b_user.rearrange("(c p e) -> p c e", c=4, p=P, e=2))
@@ -110,10 +113,10 @@ def tile_graphlearner_ib_pa_t_kernel(
             nc.sync.dma_start(out=comp[:], in_=comp_v[:, cols, :])
             feats[q] = (text, imgf, comp)
 
-        def add_nodes(s):
-            def sorted_cols(ap):
-                return ap.rearrange("p (c q e) -> p c e q", c=4, q=P, e=2)
+        def sorted_cols(ap):
+            return ap.rearrange("p (c q e) -> p c e q", c=4, q=P, e=2)
 
+        def add_nodes(s):
             for x in range(2):
                 total = work.tile([P, 4, 2, P], F32, name="total%d" % x, tag="total%d" % x)
                 sums[(s, x)] = total
@@ -122,18 +125,28 @@ def tile_graphlearner_ib_pa_t_kernel(
             for x in range(2):
                 total = sums[(s, x)]
                 n = nodes[(s, x)]
-                nc.vector.tensor_tensor(out=total[:], in0=total[:], in1=sorted_cols(n[:, 2, :]), op=ADD)
+                rest = slice(PE_QUARTERS, 4)
+                nc.vector.tensor_tensor(out=total[:, rest], in0=total[:, rest], in1=sorted_cols(n[:, 2, :])[:, rest], op=ADD)
 
         def transpose_means(s):
             mg = work.tile([P, 2, PASSES, P, 4], BF16, name="mg", tag="mg", align_bytes=64)
             grouped[s] = mg
             for x in range(2):
                 total = sums[(s, x)]
+                third = sorted_cols(nodes[(s, x)][:, 2, :])
                 for g in range(PASSES):
                     bank = tp_pool.tile([P, 4, P], F32, name="bank", tag="bank")
                     for u in range(2):
                         for e in range(2):
-                            nc.tensor.transpose(out=bank[:, 2 * u + e, :], in_=total[:, 2 * g + u, e, :], identity=ident[:])
+                            c = 2 * g + u
+                            dst = bank[:, 2 * u + e, :]
+                            if c < PE_QUARTERS:
+                                nc.tensor.matmul(out=dst, lhsT=third[:, c, e, :], rhs=ident_bf[:], start=True, stop=False)
+                                nc.tensor.matmul(
+                                    out=dst, lhsT=total[:, c, e, :], rhs=ident[:], is_transpose=True, start=False, stop=True
+                                )
+                            else:
+                                nc.tensor.transpose(out=dst, in_=total[:, c, e, :], identity=ident[:])
                     nc.scalar.activation(
                         out=mg[:, x, g, :, :], in_=bank[:].rearrange("p t r -> p r t"), func=ACT.Copy, scale=1.0 / NODES
                     )
@@ -296,8 +309,6 @@ def tile_graphlearner_ib_pa_t_kernel(
             rho, odd = divmod(s, 2)
             if s < TILES:
                 add_nodes(s)
-            if s + BASE_BUFS < TILES:
-                load_base(s + BASE_BUFS)
             if s % 4 == 1 and (s + 3) // 4 < TILES // 4:
                 load_feat((s + 3) // 4)
             if s == 0:
@@ -306,6 +317,8 @@ def tile_graphlearner_ib_pa_t_kernel(
                     nc.vector.tensor_tensor(out=bl2[:, ti, :], in0=bl_a[:], in1=bl_b[:], op=ADD)
             if 1 <= s <= TILES:
                 transpose_means(s - 1)
+                if s - 1 + BASE_BUFS < TILES:
+                    load_base(s - 1 + BASE_BUFS)
             if not odd:
                 if rho < ROUNDS:
                     transpose_feat(rho)

@@ -141,10 +141,10 @@ def tile_graphlearner_ib_pa_t_kernel(
                             c = 2 * g + u
                             dst = bank[:, 2 * u + e, :]
                             if c < PE_QUARTERS:
-                                nc.tensor.matmul(out=dst, lhsT=third[:, c, e, :], rhs=ident_bf[:], start=True, stop=False)
                                 nc.tensor.matmul(
-                                    out=dst, lhsT=total[:, c, e, :], rhs=ident[:], is_transpose=True, start=False, stop=True
+                                    out=dst, lhsT=total[:, c, e, :], rhs=ident[:], is_transpose=True, start=True, stop=False
                                 )
+                                nc.tensor.matmul(out=dst, lhsT=third[:, c, e, :], rhs=ident_bf[:], start=False, stop=True)
                             else:
                                 nc.tensor.transpose(out=dst, in_=total[:, c, e, :], identity=ident[:])
                     nc.scalar.activation(

@@ -18,7 +18,7 @@ ROUNDS = TILES // 2
 PASSES = H // (4 * P)
 CHUNKS = H // P
 BASE_BUFS = 4
-PE_QUARTERS = 3
+PE_CHUNKS = 6
 FLOPS = 2 * USERS * H * H + 4 * 2 * USERS * H * O
 
 
@@ -48,12 +48,13 @@ def tile_graphlearner_ib_pa_t_kernel(
         base_text_features.rearrange("(p t) n h -> p t n h", t=TILES),
     )
     out_v = out.rearrange("(p t) o -> p t o", t=TILES)
+    wu_v = W_user.rearrange("(j p) f -> p j f", p=P)
 
     with ExitStack() as stack:
         keep = stack.enter_context(tc.tile_pool(name="keep", bufs=1))
         base_pool = stack.enter_context(tc.tile_pool(name="base", bufs=BASE_BUFS))
         work = stack.enter_context(tc.tile_pool(name="work", bufs=2))
-        codes_pool = stack.enter_context(tc.tile_pool(name="codes", bufs=4))
+        codes_pool = stack.enter_context(tc.tile_pool(name="codes", bufs=5))
         tp_pool = stack.enter_context(tc.psum_pool(name="tp", bufs=4))
         u_pool = stack.enter_context(tc.psum_pool(name="ups", bufs=3))
         o_pool = stack.enter_context(tc.psum_pool(name="ops", bufs=1))
@@ -64,8 +65,9 @@ def tile_graphlearner_ib_pa_t_kernel(
         ident_bf = keep.tile([P, P], BF16, name="ident_bf")
         make_identity(nc, ident_bf[:])
 
-        bu_bf = keep.tile([P, 4, 2], BF16, name="bu_bf")
-        nc.scalar.dma_start(out=bu_bf[:], in_=b_user.rearrange("(c p e) -> p c e", c=4, p=P, e=2))
+        bu_rows = keep.tile([P, P], BF16, name="bu_rows")
+        nc.gpsimd.memset(bu_rows[:], 0.0)
+        nc.scalar.dma_start(out=bu_rows[0:CHUNKS, :], in_=b_user.rearrange("(j p) -> j p", p=P))
         bl_a = keep.tile([P, O], BF16, name="bl_a")
         nc.scalar.dma_start(out=bl_a[:], in_=bl_img.partition_broadcast(P))
         bl_b = keep.tile([P, O], BF16, name="bl_b")
@@ -73,26 +75,15 @@ def tile_graphlearner_ib_pa_t_kernel(
         bu = keep.tile([P, CHUNKS], F32, name="bu")
         bl2 = keep.tile([P, 2, O], F32, name="bl2")
 
-        wu_raw = keep.tile([P, 4, 2, H], BF16, name="wu_raw")
+        wu_raw = keep.tile([P, CHUNKS, H], BF16, name="wu_raw")
         ws_raw = keep.tile([P, 4, 2, H], BF16, name="ws_raw")
+        wu_grouped = keep.tile([P, CHUNKS, PASSES, 4 * P], BF16, name="wu_grouped", tag="wgroup", align_bytes=64)
         wu_codes = keep.tile([P, CHUNKS, PASSES, P], U32, name="wu_codes", align_bytes=64)
         wu_scales = keep.tile([P, CHUNKS, PASSES, P], U8, name="wu_scales", align_bytes=64)
         ws_codes = keep.tile([P, 4, PASSES, O], U32, name="ws_codes", align_bytes=64)
         ws_scales = keep.tile([P, 4, PASSES, O], U8, name="ws_scales", align_bytes=64)
 
-        nodes, feats, sums, grouped, mean_q, feat_q, planes, u_q, acc = {}, {}, {}, {}, {}, {}, {}, {}, {}
-
-        def words_out(bank):
-            return bank[:].rearrange("p (g u) r -> p g r u", u=2)
-
-        def words_in(ap):
-            return ap.bitcast(F32).rearrange("p g (r u) -> p g r u", u=2)
-
-        def transpose_words(rows):
-            bank = tp_pool.tile([P, 4, P], F32, name="bank", tag="bank")
-            for k in range(4):
-                nc.tensor.transpose(out=bank[:, k, :], in_=rows[k], identity=ident[:])
-            return bank
+        nodes, feats, sums, grouped, mean_q, feat_q, planes, u_q, acc, results = {}, {}, {}, {}, {}, {}, {}, {}, {}, {}
 
         def quantise(values, codes, scales):
             nc.vector.quantize_mx(out=codes.bitcast(FP8X4), scales=scales, in_=values)
@@ -103,50 +94,35 @@ def tile_graphlearner_ib_pa_t_kernel(
                 nc.sync.dma_start(out=t[:], in_=base_v[x][:, s])
                 nodes[(s, x)] = t
 
-        def load_feat(q):
-            cols = slice(4 * q, 4 * q + 4)
-            text = work.tile([P, 4, 256], BF16, name="text", tag="text")
-            nc.sync.dma_start(out=text[:], in_=text_v[:, cols, :])
-            imgf = work.tile([P, 4, 256], BF16, name="imgf", tag="imgf")
-            nc.sync.dma_start(out=imgf[:], in_=imgf_v[:, cols, :])
-            comp = work.tile([P, 4, 512], BF16, name="comp", tag="comp")
-            nc.sync.dma_start(out=comp[:], in_=comp_v[:, cols, :])
-            feats[q] = (text, imgf, comp)
-
-        def sorted_cols(ap):
-            return ap.rearrange("p (c q e) -> p c e q", c=4, q=P, e=2)
-
         def add_nodes(s):
+            rest = slice(P * PE_CHUNKS, H)
             for x in range(2):
-                total = work.tile([P, 4, 2, P], F32, name="total%d" % x, tag="total%d" % x)
+                total = work.tile([P, H], F32, name="total%d" % x, tag="total%d" % x)
                 sums[(s, x)] = total
                 n = nodes[(s, x)]
-                nc.vector.tensor_tensor(out=total[:], in0=sorted_cols(n[:, 0, :]), in1=sorted_cols(n[:, 1, :]), op=ADD)
+                nc.vector.tensor_tensor(out=total[:], in0=n[:, 0, :], in1=n[:, 1, :], op=ADD)
             for x in range(2):
                 total = sums[(s, x)]
-                n = nodes[(s, x)]
-                rest = slice(PE_QUARTERS, 4)
-                nc.vector.tensor_tensor(out=total[:, rest], in0=total[:, rest], in1=sorted_cols(n[:, 2, :])[:, rest], op=ADD)
+                nc.vector.tensor_tensor(out=total[:, rest], in0=total[:, rest], in1=nodes[(s, x)][:, 2, rest], op=ADD)
 
         def transpose_means(s):
             mg = work.tile([P, 2, PASSES, P, 4], BF16, name="mg", tag="mg", align_bytes=64)
             grouped[s] = mg
             for x in range(2):
                 total = sums[(s, x)]
-                third = sorted_cols(nodes[(s, x)][:, 2, :])
+                third = nodes[(s, x)][:, 2, :]
                 for g in range(PASSES):
                     bank = tp_pool.tile([P, 4, P], F32, name="bank", tag="bank")
-                    for u in range(2):
-                        for e in range(2):
-                            c = 2 * g + u
-                            dst = bank[:, 2 * u + e, :]
-                            if c < PE_QUARTERS:
-                                nc.tensor.matmul(
-                                    out=dst, lhsT=total[:, c, e, :], rhs=ident[:], is_transpose=True, start=True, stop=False
-                                )
-                                nc.tensor.matmul(out=dst, lhsT=third[:, c, e, :], rhs=ident_bf[:], start=False, stop=True)
-                            else:
-                                nc.tensor.transpose(out=dst, in_=total[:, c, e, :], identity=ident[:])
+                    for t in range(4):
+                        j = 4 * g + t
+                        cols = slice(P * j, P * (j + 1))
+                        if j < PE_CHUNKS:
+                            nc.tensor.matmul(
+                                out=bank[:, t, :], lhsT=total[:, cols], rhs=ident[:], is_transpose=True, start=True, stop=False
+                            )
+                            nc.tensor.matmul(out=bank[:, t, :], lhsT=third[:, cols], rhs=ident_bf[:], start=False, stop=True)
+                        else:
+                            nc.tensor.transpose(out=bank[:, t, :], in_=total[:, cols], identity=ident[:])
                     nc.scalar.activation(
                         out=mg[:, x, g, :, :], in_=bank[:].rearrange("p t r -> p r t"), func=ACT.Copy, scale=1.0 / NODES
                     )
@@ -161,21 +137,38 @@ def tile_graphlearner_ib_pa_t_kernel(
                 scales[:].rearrange("p x g r -> p (x g r)"),
             )
 
-        def transpose_feat(rho):
-            fg = work.tile([P, PASSES, 2, 4 * P], BF16, name="fg", tag="fg", align_bytes=64)
-            grouped[("f", rho)] = fg
-            for ti in range(2):
-                q, i = divmod(2 * rho + ti, 4)
-                text, imgf, comp = feats[q]
-                bank = transpose_words(
-                    [
-                        text[:, i, :].bitcast(F32),
-                        imgf[:, i, :].bitcast(F32),
-                        comp[:, i, 0:256].bitcast(F32),
-                        comp[:, i, 256:512].bitcast(F32),
-                    ]
-                )
-                nc.scalar.copy(out=words_in(fg[:, :, ti, :]), in_=words_out(bank))
+        def transpose_words(rows, dst):
+            bank = tp_pool.tile([P, 4, P], F32, name="bank", tag="bank")
+            for k in range(4):
+                nc.tensor.transpose(out=bank[:, k, :], in_=rows[k], identity=ident[:])
+            nc.scalar.copy(
+                out=dst.bitcast(F32).rearrange("p g (r u) -> p g r u", u=2), in_=bank[:].rearrange("p (g u) r -> p g r u", u=2)
+            )
+
+        def load_feat(q):
+            cols = slice(4 * q, 4 * q + 4)
+            text = work.tile([P, 4, 256], BF16, name="text", tag="text")
+            nc.sync.dma_start(out=text[:], in_=text_v[:, cols, :])
+            imgf = work.tile([P, 4, 256], BF16, name="imgf", tag="imgf")
+            nc.sync.dma_start(out=imgf[:], in_=imgf_v[:, cols, :])
+            comp = work.tile([P, 4, 512], BF16, name="comp", tag="comp")
+            nc.sync.dma_start(out=comp[:], in_=comp_v[:, cols, :])
+            feats[q] = (text, imgf, comp)
+
+        def transpose_feat(s):
+            rho, ti = divmod(s, 2)
+            if ti == 0:
+                fg = work.tile([P, PASSES, 2, 4 * P], BF16, name="fg", tag="fg", align_bytes=64)
+                grouped[("f", rho)] = fg
+            q, i = divmod(s, 4)
+            text, imgf, comp = feats[q]
+            rows = [
+                text[:, i, :].bitcast(F32),
+                imgf[:, i, :].bitcast(F32),
+                comp[:, i, 0:256].bitcast(F32),
+                comp[:, i, 256:512].bitcast(F32),
+            ]
+            transpose_words(rows, grouped[("f", rho)][:, :, ti, :])
 
         def quantise_feat(rho):
             codes = work.tile([P, PASSES, 2 * P], U32, name="f_codes", tag="f_codes", align_bytes=64)
@@ -188,42 +181,40 @@ def tile_graphlearner_ib_pa_t_kernel(
             )
 
         def transpose_w_user():
-            wg = keep.tile([P, CHUNKS, PASSES, 4 * P], BF16, name="wg", tag="wgroup", align_bytes=64)
-            grouped["wu"] = wg
             for j in range(CHUNKS):
-                c, e = divmod(j, 2)
-                words = wu_raw[:, c, e, :].bitcast(F32)
-                bank = transpose_words([words[:, P * k : P * (k + 1)] for k in range(4)])
-                nc.scalar.copy(out=words_in(wg[:, j, :, :]), in_=words_out(bank))
+                words = wu_raw[:, j, :].bitcast(F32)
+                transpose_words([words[:, P * k : P * (k + 1)] for k in range(4)], wu_grouped[:, j, :, :])
 
         def quantise_w_user():
-            wg = grouped["wu"]
             for half in range(2):
                 js = slice(4 * half, 4 * half + 4)
                 quantise(
-                    wg[:, js].rearrange("p j g w -> p (j g w)"),
+                    wu_grouped[:, js].rearrange("p j g w -> p (j g w)"),
                     wu_codes[:, js].rearrange("p j g r -> p (j g r)"),
                     wu_scales[:, js].rearrange("p j g r -> p (j g r)"),
                 )
 
-        def transpose_w_out():
-            sg = keep.tile([P, 4, PASSES, 2, 4 * P], BF16, name="sg", tag="wgroup", align_bytes=64)
-            grouped["ws"] = sg
-            for m in range(4):
-                for a in range(2):
-                    words = ws_raw[:, m, a, :].bitcast(F32)
-                    bank = transpose_words([words[:, P * k : P * (k + 1)] for k in range(4)])
-                    nc.scalar.copy(out=words_in(sg[:, m, :, a, :]), in_=words_out(bank))
-
-        def quantise_w_out():
+        def transpose_w_out(half):
+            if half == 0:
+                sg = keep.tile([P, 4, PASSES, 2, P, 4], BF16, name="sg", tag="wgroup", align_bytes=64)
+                grouped["ws"] = sg
             sg = grouped["ws"]
-            for half in range(2):
-                ms = slice(2 * half, 2 * half + 2)
-                quantise(
-                    sg[:, ms].rearrange("p m g a w -> p (m g a w)"),
-                    ws_codes[:, ms].rearrange("p m g o -> p (m g o)"),
-                    ws_scales[:, ms].rearrange("p m g o -> p (m g o)"),
-                )
+            for m in (2 * half, 2 * half + 1):
+                for a in range(2):
+                    for g in range(PASSES):
+                        bank = tp_pool.tile([P, 4, P], BF16, name="bank_bf", tag="bank")
+                        for t in range(4):
+                            j = 4 * g + t
+                            nc.tensor.transpose(out=bank[:, t, :], in_=ws_raw[:, m, a, P * j : P * (j + 1)], identity=ident_bf[:])
+                        nc.scalar.copy(out=sg[:, m, g, a, :, :], in_=bank[:].rearrange("p t r -> p r t"))
+
+        def quantise_w_out(half):
+            ms = slice(2 * half, 2 * half + 2)
+            quantise(
+                grouped["ws"][:, ms].rearrange("p m g a r t -> p (m g a r t)"),
+                ws_codes[:, ms].rearrange("p m g o -> p (m g o)"),
+                ws_scales[:, ms].rearrange("p m g o -> p (m g o)"),
+            )
 
         def stage1(rho):
             codes, scales = feat_q[rho]
@@ -290,59 +281,73 @@ def tile_graphlearner_ib_pa_t_kernel(
                         stop=(i == len(left) - 1),
                     )
 
-        def finish(rho):
+        def add_bias(rho):
             res = work.tile([P, 2, O], F32, name="res", tag="res")
+            results[rho] = res
             nc.vector.tensor_tensor(out=res[:], in0=acc[rho][:], in1=bl2[:], op=ADD)
-            nc.scalar.activation(out=res[:], in_=res[:], func=ACT.Relu)
-            nc.scalar.dma_start(out=out_v[:, 2 * rho : 2 * rho + 2, :], in_=res[:])
+
+        def relu(rho):
+            nc.vector.tensor_scalar_max(out=results[rho][:], in0=results[rho][:], scalar1=0.0)
+
+        def store(rho):
+            nc.sync.dma_start(out=out_v[:, 2 * rho : 2 * rho + 2, :], in_=results[rho][:])
 
         load_base(0)
         load_feat(0)
-        nc.sync.dma_start(out=wu_raw[:], in_=W_user.rearrange("(c p e) f -> p c e f", c=4, p=P, e=2))
+        for i in range(4):
+            nc.sync.dma_start(out=wu_raw[:, 2 * i : 2 * i + 2, :], in_=wu_v[:, 2 * i : 2 * i + 2, :])
         load_base(1)
         load_base(2)
         for m, w in enumerate((Wl_img, Wr_img, Wl_txt, Wr_txt)):
             nc.sync.dma_start(out=ws_raw[:, m], in_=w.rearrange("(a p) h -> p a h", a=2))
         load_base(3)
 
-        for s in range(TILES + 3):
-            rho, odd = divmod(s, 2)
-            if s < TILES:
+        def tile_at(s):
+            return 0 <= s < TILES
+
+        def round_at(twice):
+            return twice // 2 if twice % 2 == 0 and 0 <= twice // 2 < ROUNDS else None
+
+        for s in range(-1, TILES + 8):
+            if round_at(s - 7) is not None:
+                store(round_at(s - 7))
+            if tile_at(s):
                 add_nodes(s)
-            if s % 4 == 1 and (s + 3) // 4 < TILES // 4:
-                load_feat((s + 3) // 4)
+            if round_at(s - 6) is not None:
+                add_bias(round_at(s - 6))
             if s == 0:
-                nc.vector.tensor_copy(out=bu[:], in_=bu_bf[:].rearrange("p c e -> p (c e)"))
+                bu_t = tp_pool.tile([P, P], BF16, name="bu_t", tag="bank")
+                nc.tensor.transpose(out=bu_t[:], in_=bu_rows[:], identity=ident_bf[:])
+                nc.vector.tensor_copy(out=bu[:], in_=bu_t[:, 0:CHUNKS])
                 for ti in range(2):
                     nc.vector.tensor_tensor(out=bl2[:, ti, :], in0=bl_a[:], in1=bl_b[:], op=ADD)
-            if 1 <= s <= TILES:
+            if tile_at(s - 1):
                 transpose_means(s - 1)
                 if s - 1 + BASE_BUFS < TILES:
                     load_base(s - 1 + BASE_BUFS)
-            if not odd:
-                if rho < ROUNDS:
-                    transpose_feat(rho)
-                if s == 0:
-                    transpose_w_user()
-                if s == 2:
-                    transpose_w_out()
-            else:
-                if rho < ROUNDS:
-                    stage1(rho)
-                if 1 <= rho <= ROUNDS:
-                    stage2(rho - 1)
-            if not odd and 1 <= rho <= ROUNDS:
-                regroup_u(rho - 1)
-            if 1 <= s <= TILES:
-                quantise_means(s - 1)
-            if not odd:
-                if s == 0:
-                    quantise_w_user()
-                if 1 <= rho <= ROUNDS:
-                    quantise_u(rho - 1)
-                if rho < ROUNDS:
-                    quantise_feat(rho)
-                if s == 2:
-                    quantise_w_out()
-                if 2 <= rho <= ROUNDS + 1:
-                    finish(rho - 2)
+            if tile_at(s + 1):
+                transpose_feat(s + 1)
+            if s % 4 == 0 and 1 <= s // 4 + 1 < TILES // 4:
+                load_feat(s // 4 + 1)
+            if s == 0:
+                transpose_w_user()
+            if s in (2, 3):
+                transpose_w_out(s - 2)
+            if round_at(s - 5) is not None:
+                stage2(round_at(s - 5))
+            if round_at(s - 2) is not None:
+                stage1(round_at(s - 2))
+            if tile_at(s - 2):
+                quantise_means(s - 2)
+            if round_at(s - 1) is not None:
+                quantise_feat(round_at(s - 1))
+            if s == 1:
+                quantise_w_user()
+            if s in (3, 4):
+                quantise_w_out(s - 3)
+            if round_at(s - 3) is not None:
+                regroup_u(round_at(s - 3))
+            if round_at(s - 4) is not None:
+                quantise_u(round_at(s - 4))
+            if round_at(s - 6) is not None:
+                relu(round_at(s - 6))

@@ -105,27 +105,28 @@ def tile_graphlearner_ib_pa_t_kernel(
                 total = sums[(s, x)]
                 nc.vector.tensor_tensor(out=total[:, rest], in0=total[:, rest], in1=nodes[(s, x)][:, 2, rest], op=ADD)
 
-        def transpose_means(s):
-            mg = work.tile([P, 2, PASSES, P, 4], BF16, name="mg", tag="mg", align_bytes=64)
-            grouped[s] = mg
-            for x in range(2):
-                total = sums[(s, x)]
-                third = nodes[(s, x)][:, 2, :]
-                for g in range(PASSES):
-                    bank = tp_pool.tile([P, 4, P], F32, name="bank", tag="bank")
-                    for t in range(4):
-                        j = 4 * g + t
-                        cols = slice(P * j, P * (j + 1))
-                        if j < PE_CHUNKS:
-                            nc.tensor.matmul(
-                                out=bank[:, t, :], lhsT=total[:, cols], rhs=ident[:], is_transpose=True, start=True, stop=False
-                            )
-                            nc.tensor.matmul(out=bank[:, t, :], lhsT=third[:, cols], rhs=ident_bf[:], start=False, stop=True)
-                        else:
-                            nc.tensor.transpose(out=bank[:, t, :], in_=total[:, cols], identity=ident[:])
-                    nc.scalar.activation(
-                        out=mg[:, x, g, :, :], in_=bank[:].rearrange("p t r -> p r t"), func=ACT.Copy, scale=1.0 / NODES
-                    )
+        def transpose_means(s, x):
+            if x == 0:
+                mg = work.tile([P, 2, PASSES, P, 4], BF16, name="mg", tag="mg", align_bytes=64)
+                grouped[s] = mg
+            mg = grouped[s]
+            total = sums[(s, x)]
+            third = nodes[(s, x)][:, 2, :]
+            for g in range(PASSES):
+                bank = tp_pool.tile([P, 4, P], F32, name="bank", tag="bank")
+                for t in range(4):
+                    j = 4 * g + t
+                    cols = slice(P * j, P * (j + 1))
+                    if j < PE_CHUNKS:
+                        nc.tensor.matmul(
+                            out=bank[:, t, :], lhsT=total[:, cols], rhs=ident[:], is_transpose=True, start=True, stop=False
+                        )
+                        nc.tensor.matmul(out=bank[:, t, :], lhsT=third[:, cols], rhs=ident_bf[:], start=False, stop=True)
+                    else:
+                        nc.tensor.transpose(out=bank[:, t, :], in_=total[:, cols], identity=ident[:])
+                nc.scalar.activation(
+                    out=mg[:, x, g, :, :], in_=bank[:].rearrange("p t r -> p r t"), func=ACT.Copy, scale=1.0 / NODES
+                )
 
         def quantise_means(s):
             codes = codes_pool.tile([P, 2, PASSES, P], U32, name="m_codes", tag="m_codes", align_bytes=64)
@@ -216,11 +217,13 @@ def tile_graphlearner_ib_pa_t_kernel(
                 ws_scales[:, ms].rearrange("p m g o -> p (m g o)"),
             )
 
-        def stage1(rho):
+        def stage1(rho, half):
             codes, scales = feat_q[rho]
-            up = work.tile([P, CHUNKS, 2 * P], BF16, name="up", tag="up")
-            planes[rho] = up
-            for b in range(CHUNKS // 2):
+            if half == 0:
+                up = work.tile([P, CHUNKS, 2 * P], BF16, name="up", tag="up")
+                planes[rho] = up
+            up = planes[rho]
+            for b in (2 * half, 2 * half + 1):
                 ub = u_pool.tile([P, 2, 2 * P], F32, name="ub", tag="ub")
                 for jj in range(2):
                     j = 2 * b + jj
@@ -257,29 +260,30 @@ def tile_graphlearner_ib_pa_t_kernel(
                 scales[:].rearrange("p g n -> p (g n)"),
             )
 
-        def stage2(rho):
-            ob = o_pool.tile([P, 2, O], F32, name="ob", tag="ob")
-            acc[rho] = ob
+        def stage2(rho, ti):
+            if ti == 0:
+                ob = o_pool.tile([P, 2, O], F32, name="ob", tag="ob")
+                acc[rho] = ob
+            ob = acc[rho]
             u_codes, u_scales = u_q[rho]
-            for ti in range(2):
-                m_codes, m_scales = mean_q[2 * rho + ti]
-                cols = slice(P * ti, P * (ti + 1))
-                left = []
-                for g in range(PASSES):
-                    left.append((m_codes[:, 0, g, :], m_scales[:, 0, g, :], 0, g))
-                    left.append((u_codes[:, g, cols], u_scales[:, g, cols], 1, g))
-                    left.append((m_codes[:, 1, g, :], m_scales[:, 1, g, :], 2, g))
-                    left.append((u_codes[:, g, cols], u_scales[:, g, cols], 3, g))
-                for i, (codes, scales, m, g) in enumerate(left):
-                    nc.tensor.matmul_mx(
-                        out=ob[:, ti, :],
-                        lhsT=codes.bitcast(FP8X4),
-                        lhsT_scale=scales,
-                        rhs=ws_codes[:, m, g, :].bitcast(FP8X4),
-                        rhs_scale=ws_scales[:, m, g, :],
-                        start=(i == 0),
-                        stop=(i == len(left) - 1),
-                    )
+            m_codes, m_scales = mean_q[2 * rho + ti]
+            cols = slice(P * ti, P * (ti + 1))
+            left = []
+            for g in range(PASSES):
+                left.append((m_codes[:, 0, g, :], m_scales[:, 0, g, :], 0, g))
+                left.append((u_codes[:, g, cols], u_scales[:, g, cols], 1, g))
+                left.append((m_codes[:, 1, g, :], m_scales[:, 1, g, :], 2, g))
+                left.append((u_codes[:, g, cols], u_scales[:, g, cols], 3, g))
+            for i, (codes, scales, m, g) in enumerate(left):
+                nc.tensor.matmul_mx(
+                    out=ob[:, ti, :],
+                    lhsT=codes.bitcast(FP8X4),
+                    lhsT_scale=scales,
+                    rhs=ws_codes[:, m, g, :].bitcast(FP8X4),
+                    rhs_scale=ws_scales[:, m, g, :],
+                    start=(i == 0),
+                    stop=(i == len(left) - 1),
+                )
 
         def add_bias(rho):
             res = work.tile([P, 2, O], F32, name="res", tag="res")
@@ -321,22 +325,24 @@ def tile_graphlearner_ib_pa_t_kernel(
                 nc.vector.tensor_copy(out=bu[:], in_=bu_t[:, 0:CHUNKS])
                 for ti in range(2):
                     nc.vector.tensor_tensor(out=bl2[:, ti, :], in0=bl_a[:], in1=bl_b[:], op=ADD)
-            if tile_at(s - 1):
-                transpose_means(s - 1)
-                if s - 1 + BASE_BUFS < TILES:
-                    load_base(s - 1 + BASE_BUFS)
-            if tile_at(s + 1):
-                transpose_feat(s + 1)
-            if s % 4 == 0 and 1 <= s // 4 + 1 < TILES // 4:
-                load_feat(s // 4 + 1)
-            if s == 0:
-                transpose_w_user()
-            if s in (2, 3):
-                transpose_w_out(s - 2)
-            if round_at(s - 5) is not None:
-                stage2(round_at(s - 5))
-            if round_at(s - 2) is not None:
-                stage1(round_at(s - 2))
+            for half in range(2):
+                if tile_at(s - 1):
+                    transpose_means(s - 1, half)
+                if half == 1:
+                    if tile_at(s - 1) and s - 1 + BASE_BUFS < TILES:
+                        load_base(s - 1 + BASE_BUFS)
+                    if tile_at(s + 1):
+                        transpose_feat(s + 1)
+                    if s % 4 == 0 and 1 <= s // 4 + 1 < TILES // 4:
+                        load_feat(s // 4 + 1)
+                    if s == 0:
+                        transpose_w_user()
+                    if s in (2, 3):
+                        transpose_w_out(s - 2)
+                if round_at(s - 5) is not None:
+                    stage2(round_at(s - 5), half)
+                if round_at(s - 2) is not None:
+                    stage1(round_at(s - 2), half)
             if tile_at(s - 2):
                 quantise_means(s - 2)
             if round_at(s - 1) is not None:

@@ -55,9 +55,7 @@ def tile_graphlearner_ib_pa_t_kernel(
         base_pool = stack.enter_context(tc.tile_pool(name="base", bufs=BASE_BUFS))
         work = stack.enter_context(tc.tile_pool(name="work", bufs=2))
         codes_pool = stack.enter_context(tc.tile_pool(name="codes", bufs=5))
-        tp_pool = stack.enter_context(tc.psum_pool(name="tp", bufs=4))
-        u_pool = stack.enter_context(tc.psum_pool(name="ups", bufs=3))
-        o_pool = stack.enter_context(tc.psum_pool(name="ops", bufs=1))
+        psum = stack.enter_context(tc.psum_pool(name="psum", bufs=8))
         stack.enter_context(tc.manual_schedule())
 
         ident = keep.tile([P, P], F32, name="ident")
@@ -105,28 +103,27 @@ def tile_graphlearner_ib_pa_t_kernel(
                 total = sums[(s, x)]
                 nc.vector.tensor_tensor(out=total[:, rest], in0=total[:, rest], in1=nodes[(s, x)][:, 2, rest], op=ADD)
 
-        def transpose_means(s, x):
-            if x == 0:
-                mg = work.tile([P, 2, PASSES, P, 4], BF16, name="mg", tag="mg", align_bytes=64)
-                grouped[s] = mg
-            mg = grouped[s]
-            total = sums[(s, x)]
-            third = nodes[(s, x)][:, 2, :]
-            for g in range(PASSES):
-                bank = tp_pool.tile([P, 4, P], F32, name="bank", tag="bank")
-                for t in range(4):
-                    j = 4 * g + t
-                    cols = slice(P * j, P * (j + 1))
-                    if j < PE_CHUNKS:
-                        nc.tensor.matmul(
-                            out=bank[:, t, :], lhsT=total[:, cols], rhs=ident[:], is_transpose=True, start=True, stop=False
-                        )
-                        nc.tensor.matmul(out=bank[:, t, :], lhsT=third[:, cols], rhs=ident_bf[:], start=False, stop=True)
-                    else:
-                        nc.tensor.transpose(out=bank[:, t, :], in_=total[:, cols], identity=ident[:])
-                nc.scalar.activation(
-                    out=mg[:, x, g, :, :], in_=bank[:].rearrange("p t r -> p r t"), func=ACT.Copy, scale=1.0 / NODES
-                )
+        def transpose_means(s):
+            mg = work.tile([P, 2, PASSES, P, 4], BF16, name="mg", tag="mg", align_bytes=64)
+            grouped[s] = mg
+            for x in range(2):
+                total = sums[(s, x)]
+                third = nodes[(s, x)][:, 2, :]
+                for g in range(PASSES):
+                    bank = psum.tile([P, 4, P], F32, name="bank", tag="bank")
+                    for t in range(4):
+                        j = 4 * g + t
+                        cols = slice(P * j, P * (j + 1))
+                        if j < PE_CHUNKS:
+                            nc.tensor.matmul(
+                                out=bank[:, t, :], lhsT=total[:, cols], rhs=ident[:], is_transpose=True, start=True, stop=False
+                            )
+                            nc.tensor.matmul(out=bank[:, t, :], lhsT=third[:, cols], rhs=ident_bf[:], start=False, stop=True)
+                        else:
+                            nc.tensor.transpose(out=bank[:, t, :], in_=total[:, cols], identity=ident[:])
+                    nc.scalar.activation(
+                        out=mg[:, x, g, :, :], in_=bank[:].rearrange("p t r -> p r t"), func=ACT.Copy, scale=1.0 / NODES
+                    )
 
         def quantise_means(s):
             codes = codes_pool.tile([P, 2, PASSES, P], U32, name="m_codes", tag="m_codes", align_bytes=64)
@@ -139,7 +136,7 @@ def tile_graphlearner_ib_pa_t_kernel(
             )
 
         def transpose_words(rows, dst):
-            bank = tp_pool.tile([P, 4, P], F32, name="bank", tag="bank")
+            bank = psum.tile([P, 4, P], F32, name="bank", tag="bank")
             for k in range(4):
                 nc.tensor.transpose(out=bank[:, k, :], in_=rows[k], identity=ident[:])
             nc.scalar.copy(
@@ -203,7 +200,7 @@ def tile_graphlearner_ib_pa_t_kernel(
             for m in (2 * half, 2 * half + 1):
                 for a in range(2):
                     for g in range(PASSES):
-                        bank = tp_pool.tile([P, 4, P], BF16, name="bank_bf", tag="bank")
+                        bank = psum.tile([P, 4, P], BF16, name="bank_bf", tag="bank")
                         for t in range(4):
                             j = 4 * g + t
                             nc.tensor.transpose(out=bank[:, t, :], in_=ws_raw[:, m, a, P * j : P * (j + 1)], identity=ident_bf[:])
@@ -217,14 +214,12 @@ def tile_graphlearner_ib_pa_t_kernel(
                 ws_scales[:, ms].rearrange("p m g o -> p (m g o)"),
             )
 
-        def stage1(rho, half):
+        def stage1(rho):
             codes, scales = feat_q[rho]
-            if half == 0:
-                up = work.tile([P, CHUNKS, 2 * P], BF16, name="up", tag="up")
-                planes[rho] = up
-            up = planes[rho]
-            for b in (2 * half, 2 * half + 1):
-                ub = u_pool.tile([P, 2, 2 * P], F32, name="ub", tag="ub")
+            up = work.tile([P, CHUNKS, 2 * P], BF16, name="up", tag="up")
+            planes[rho] = up
+            for b in range(CHUNKS // 2):
+                ub = psum.tile([P, 2, 2 * P], F32, name="ub", tag="bank")
                 for jj in range(2):
                     j = 2 * b + jj
                     for g in range(PASSES):
@@ -260,30 +255,29 @@ def tile_graphlearner_ib_pa_t_kernel(
                 scales[:].rearrange("p g n -> p (g n)"),
             )
 
-        def stage2(rho, ti):
-            if ti == 0:
-                ob = o_pool.tile([P, 2, O], F32, name="ob", tag="ob")
-                acc[rho] = ob
-            ob = acc[rho]
+        def stage2(rho):
+            ob = psum.tile([P, 2, O], F32, name="ob", tag="bank")
+            acc[rho] = ob
             u_codes, u_scales = u_q[rho]
-            m_codes, m_scales = mean_q[2 * rho + ti]
-            cols = slice(P * ti, P * (ti + 1))
-            left = []
-            for g in range(PASSES):
-                left.append((m_codes[:, 0, g, :], m_scales[:, 0, g, :], 0, g))
-                left.append((u_codes[:, g, cols], u_scales[:, g, cols], 1, g))
-                left.append((m_codes[:, 1, g, :], m_scales[:, 1, g, :], 2, g))
-                left.append((u_codes[:, g, cols], u_scales[:, g, cols], 3, g))
-            for i, (codes, scales, m, g) in enumerate(left):
-                nc.tensor.matmul_mx(
-                    out=ob[:, ti, :],
-                    lhsT=codes.bitcast(FP8X4),
-                    lhsT_scale=scales,
-                    rhs=ws_codes[:, m, g, :].bitcast(FP8X4),
-                    rhs_scale=ws_scales[:, m, g, :],
-                    start=(i == 0),
-                    stop=(i == len(left) - 1),
-                )
+            for ti in range(2):
+                m_codes, m_scales = mean_q[2 * rho + ti]
+                cols = slice(P * ti, P * (ti + 1))
+                left = []
+                for g in range(PASSES):
+                    left.append((m_codes[:, 0, g, :], m_scales[:, 0, g, :], 0, g))
+                    left.append((u_codes[:, g, cols], u_scales[:, g, cols], 1, g))
+                    left.append((m_codes[:, 1, g, :], m_scales[:, 1, g, :], 2, g))
+                    left.append((u_codes[:, g, cols], u_scales[:, g, cols], 3, g))
+                for i, (codes, scales, m, g) in enumerate(left):
+                    nc.tensor.matmul_mx(
+                        out=ob[:, ti, :],
+                        lhsT=codes.bitcast(FP8X4),
+                        lhsT_scale=scales,
+                        rhs=ws_codes[:, m, g, :].bitcast(FP8X4),
+                        rhs_scale=ws_scales[:, m, g, :],
+                        start=(i == 0),
+                        stop=(i == len(left) - 1),
+                    )
 
         def add_bias(rho):
             res = work.tile([P, 2, O], F32, name="res", tag="res")
@@ -320,29 +314,27 @@ def tile_graphlearner_ib_pa_t_kernel(
             if round_at(s - 6) is not None:
                 add_bias(round_at(s - 6))
             if s == 0:
-                bu_t = tp_pool.tile([P, P], BF16, name="bu_t", tag="bank")
+                bu_t = psum.tile([P, P], BF16, name="bu_t", tag="bank")
                 nc.tensor.transpose(out=bu_t[:], in_=bu_rows[:], identity=ident_bf[:])
                 nc.vector.tensor_copy(out=bu[:], in_=bu_t[:, 0:CHUNKS])
                 for ti in range(2):
                     nc.vector.tensor_tensor(out=bl2[:, ti, :], in0=bl_a[:], in1=bl_b[:], op=ADD)
-            for half in range(2):
-                if tile_at(s - 1):
-                    transpose_means(s - 1, half)
-                if half == 1:
-                    if tile_at(s - 1) and s - 1 + BASE_BUFS < TILES:
-                        load_base(s - 1 + BASE_BUFS)
-                    if tile_at(s + 1):
-                        transpose_feat(s + 1)
-                    if s % 4 == 0 and 1 <= s // 4 + 1 < TILES // 4:
-                        load_feat(s // 4 + 1)
-                    if s == 0:
-                        transpose_w_user()
-                    if s in (2, 3):
-                        transpose_w_out(s - 2)
-                if round_at(s - 5) is not None:
-                    stage2(round_at(s - 5), half)
-                if round_at(s - 2) is not None:
-                    stage1(round_at(s - 2), half)
+            if tile_at(s - 1):
+                transpose_means(s - 1)
+                if s - 1 + BASE_BUFS < TILES:
+                    load_base(s - 1 + BASE_BUFS)
+            if tile_at(s + 1):
+                transpose_feat(s + 1)
+            if s % 4 == 0 and 1 <= s // 4 + 1 < TILES // 4:
+                load_feat(s // 4 + 1)
+            if s == 0:
+                transpose_w_user()
+            if s in (2, 3):
+                transpose_w_out(s - 2)
+            if round_at(s - 5) is not None:
+                stage2(round_at(s - 5))
+            if round_at(s - 2) is not None:
+                stage1(round_at(s - 2))
             if tile_at(s - 2):
                 quantise_means(s - 2)
             if round_at(s - 1) is not None:

@@ -106,24 +106,30 @@ def tile_graphlearner_ib_pa_t_kernel(
         def transpose_means(s):
             mg = work.tile([P, 2, PASSES, P, 4], BF16, name="mg", tag="mg", align_bytes=64)
             grouped[s] = mg
+            banks = {}
             for x in range(2):
-                total = sums[(s, x)]
-                third = nodes[(s, x)][:, 2, :]
                 for g in range(PASSES):
                     bank = psum.tile([P, 4, P], F32, name="bank", tag="bank")
-                    for t in range(4):
-                        j = 4 * g + t
-                        cols = slice(P * j, P * (j + 1))
-                        if j < PE_CHUNKS:
-                            nc.tensor.matmul(
-                                out=bank[:, t, :], lhsT=total[:, cols], rhs=ident[:], is_transpose=True, start=True, stop=False
-                            )
-                            nc.tensor.matmul(out=bank[:, t, :], lhsT=third[:, cols], rhs=ident_bf[:], start=False, stop=True)
-                        else:
-                            nc.tensor.transpose(out=bank[:, t, :], in_=total[:, cols], identity=ident[:])
-                    nc.scalar.activation(
-                        out=mg[:, x, g, :, :], in_=bank[:].rearrange("p t r -> p r t"), func=ACT.Copy, scale=1.0 / NODES
+                    banks[(x, g)] = bank
+            for t in range(4):
+                for (x, g), bank in banks.items():
+                    cols = slice(P * (4 * g + t), P * (4 * g + t + 1))
+                    nc.tensor.matmul(
+                        out=bank[:, t, :],
+                        lhsT=sums[(s, x)][:, cols],
+                        rhs=ident[:],
+                        is_transpose=True,
+                        start=True,
+                        stop=(4 * g + t >= PE_CHUNKS),
                     )
+                for (x, g), bank in banks.items():
+                    cols = slice(P * (4 * g + t), P * (4 * g + t + 1))
+                    if 4 * g + t < PE_CHUNKS:
+                        nc.tensor.matmul(out=bank[:, t, :], lhsT=nodes[(s, x)][:, 2, cols], rhs=ident_bf[:], start=False, stop=True)
+            for (x, g), bank in banks.items():
+                nc.scalar.activation(
+                    out=mg[:, x, g, :, :], in_=bank[:].rearrange("p t r -> p r t"), func=ACT.Copy, scale=1.0 / NODES
+                )
 
         def quantise_means(s):
             codes = codes_pool.tile([P, 2, PASSES, P], U32, name="m_codes", tag="m_codes", align_bytes=64)

@@ -106,30 +106,28 @@ def tile_graphlearner_ib_pa_t_kernel(
         def transpose_means(s):
             mg = work.tile([P, 2, PASSES, P, 4], BF16, name="mg", tag="mg", align_bytes=64)
             grouped[s] = mg
-            banks = {}
             for x in range(2):
+                total = sums[(s, x)]
+                third = nodes[(s, x)][:, 2, :]
                 for g in range(PASSES):
                     bank = psum.tile([P, 4, P], F32, name="bank", tag="bank")
-                    banks[(x, g)] = bank
-            for t in range(4):
-                for (x, g), bank in banks.items():
-                    cols = slice(P * (4 * g + t), P * (4 * g + t + 1))
-                    nc.tensor.matmul(
-                        out=bank[:, t, :],
-                        lhsT=sums[(s, x)][:, cols],
-                        rhs=ident[:],
-                        is_transpose=True,
-                        start=True,
-                        stop=(4 * g + t >= PE_CHUNKS),
+                    added = [t for t in range(4) if 4 * g + t < PE_CHUNKS]
+                    for t in range(4):
+                        cols = slice(P * (4 * g + t), P * (4 * g + t + 1))
+                        nc.tensor.matmul(
+                            out=bank[:, t, :],
+                            lhsT=total[:, cols],
+                            rhs=ident[:],
+                            is_transpose=True,
+                            start=(t == 0),
+                            stop=(t == 3 and not added),
+                        )
+                    for t in added:
+                        cols = slice(P * (4 * g + t), P * (4 * g + t + 1))
+                        nc.tensor.matmul(out=bank[:, t, :], lhsT=third[:, cols], rhs=ident_bf[:], start=False, stop=(t == added[-1]))
+                    nc.scalar.activation(
+                        out=mg[:, x, g, :, :], in_=bank[:].rearrange("p t r -> p r t"), func=ACT.Copy, scale=1.0 / NODES
                     )
-                for (x, g), bank in banks.items():
-                    cols = slice(P * (4 * g + t), P * (4 * g + t + 1))
-                    if 4 * g + t < PE_CHUNKS:
-                        nc.tensor.matmul(out=bank[:, t, :], lhsT=nodes[(s, x)][:, 2, cols], rhs=ident_bf[:], start=False, stop=True)
-            for (x, g), bank in banks.items():
-                nc.scalar.activation(
-                    out=mg[:, x, g, :, :], in_=bank[:].rearrange("p t r -> p r t"), func=ACT.Copy, scale=1.0 / NODES
-                )
 
         def quantise_means(s):
             codes = codes_pool.tile([P, 2, PASSES, P], U32, name="m_codes", tag="m_codes", align_bytes=64)

from contextlib import ExitStack

import concourse.mybir as mybir
from concourse.masks import make_identity

F32 = mybir.dt.float32
BF16 = mybir.dt.bfloat16
U32 = mybir.dt.uint32
U8 = mybir.dt.uint8
FP8X4 = mybir.dt.float8_e4m3fn_x4
ACT = mybir.ActivationFunctionType
ADD = mybir.AluOpType.add

P = 128
USERS, NODES, H, O = 2048, 3, 1024, 256
TILES = USERS // P
ROUNDS = TILES // 2
PASSES = H // (4 * P)
CHUNKS = H // P
BASE_BUFS = 4
PE_CHUNKS = 6
FLOPS = 2 * USERS * H * H + 4 * 2 * USERS * H * O


def tile_graphlearner_ib_pa_t_kernel(
    tc,
    input_text,
    input_img,
    input_compress,
    base_text_features,
    base_img_features,
    W_user,
    b_user,
    Wl_img,
    bl_img,
    Wr_img,
    Wl_txt,
    bl_txt,
    Wr_txt,
    out,
):
    nc = tc.nc
    text_v = input_text.rearrange("(p t) o d -> p t (o d)", t=TILES)
    imgf_v = input_img.rearrange("(p t) o d -> p t (o d)", t=TILES)
    comp_v = input_compress.rearrange("(p t) d -> p t d", t=TILES)
    base_v = (
        base_img_features.rearrange("(p t) n h -> p t n h", t=TILES),
        base_text_features.rearrange("(p t) n h -> p t n h", t=TILES),
    )
    out_v = out.rearrange("(p t) o -> p t o", t=TILES)
    wu_v = W_user.rearrange("(j p) f -> p j f", p=P)

    with ExitStack() as stack:
        keep = stack.enter_context(tc.tile_pool(name="keep", bufs=1))
        base_pool = stack.enter_context(tc.tile_pool(name="base", bufs=BASE_BUFS))
        work = stack.enter_context(tc.tile_pool(name="work", bufs=2))
        codes_pool = stack.enter_context(tc.tile_pool(name="codes", bufs=5))
        psum = stack.enter_context(tc.psum_pool(name="psum", bufs=8))
        stack.enter_context(tc.manual_schedule())

        ident = keep.tile([P, P], F32, name="ident")
        make_identity(nc, ident[:])
        ident_bf = keep.tile([P, P], BF16, name="ident_bf")
        make_identity(nc, ident_bf[:])

        bu_rows = keep.tile([P, P], BF16, name="bu_rows")
        nc.gpsimd.memset(bu_rows[:], 0.0)
        nc.scalar.dma_start(out=bu_rows[0:CHUNKS, :], in_=b_user.rearrange("(j p) -> j p", p=P))
        bl_a = keep.tile([P, O], BF16, name="bl_a")
        nc.scalar.dma_start(out=bl_a[:], in_=bl_img.partition_broadcast(P))
        bl_b = keep.tile([P, O], BF16, name="bl_b")
        nc.scalar.dma_start(out=bl_b[:], in_=bl_txt.partition_broadcast(P))
        bu = keep.tile([P, CHUNKS], F32, name="bu")
        bl2 = keep.tile([P, 2, O], F32, name="bl2")

        wu_raw = keep.tile([P, CHUNKS, H], BF16, name="wu_raw")
        ws_raw = keep.tile([P, 4, 2, H], BF16, name="ws_raw")
        wu_grouped = keep.tile([P, CHUNKS, PASSES, 4 * P], BF16, name="wu_grouped", tag="wgroup", align_bytes=64)
        wu_codes = keep.tile([P, CHUNKS, PASSES, P], U32, name="wu_codes", align_bytes=64)
        wu_scales = keep.tile([P, CHUNKS, PASSES, P], U8, name="wu_scales", align_bytes=64)
        ws_codes = keep.tile([P, 4, PASSES, O], U32, name="ws_codes", align_bytes=64)
        ws_scales = keep.tile([P, 4, PASSES, O], U8, name="ws_scales", align_bytes=64)

        nodes, feats, sums, grouped, mean_q, feat_q, planes, u_q, acc, results = {}, {}, {}, {}, {}, {}, {}, {}, {}, {}

        def quantise(values, codes, scales):
            nc.vector.quantize_mx(out=codes.bitcast(FP8X4), scales=scales, in_=values)

        def load_base(s):
            for x in range(2):
                t = base_pool.tile([P, NODES, H], BF16, name="nodes%d" % x, tag="nodes%d" % x)
                nc.sync.dma_start(out=t[:], in_=base_v[x][:, s])
                nodes[(s, x)] = t

        def add_nodes(s):
            rest = slice(P * PE_CHUNKS, H)
            for x in range(2):
                total = work.tile([P, H], F32, name="total%d" % x, tag="total%d" % x)
                sums[(s, x)] = total
                n = nodes[(s, x)]
                nc.vector.tensor_tensor(out=total[:], in0=n[:, 0, :], in1=n[:, 1, :], op=ADD)
            for x in range(2):
                total = sums[(s, x)]
                nc.vector.tensor_tensor(out=total[:, rest], in0=total[:, rest], in1=nodes[(s, x)][:, 2, rest], op=ADD)

        def transpose_means(s):
            mg = work.tile([P, 2, PASSES, P, 4], BF16, name="mg", tag="mg", align_bytes=64)
            grouped[s] = mg
            for x in range(2):
                total = sums[(s, x)]
                third = nodes[(s, x)][:, 2, :]
                for g in range(PASSES):
                    bank = psum.tile([P, 4, P], F32, name="bank", tag="bank")
                    added = [t for t in range(4) if 4 * g + t < PE_CHUNKS]
                    for t in range(4):
                        cols = slice(P * (4 * g + t), P * (4 * g + t + 1))
                        nc.tensor.matmul(
                            out=bank[:, t, :],
                            lhsT=total[:, cols],
                            rhs=ident[:],
                            is_transpose=True,
                            start=(t == 0),
                            stop=(t == 3 and not added),
                        )
                    for t in added:
                        cols = slice(P * (4 * g + t), P * (4 * g + t + 1))
                        nc.tensor.matmul(out=bank[:, t, :], lhsT=third[:, cols], rhs=ident_bf[:], start=False, stop=(t == added[-1]))
                    nc.scalar.activation(
                        out=mg[:, x, g, :, :], in_=bank[:].rearrange("p t r -> p r t"), func=ACT.Copy, scale=1.0 / NODES
                    )

        def quantise_means(s):
            codes = codes_pool.tile([P, 2, PASSES, P], U32, name="m_codes", tag="m_codes", align_bytes=64)
            scales = codes_pool.tile([P, 2, PASSES, P], U8, name="m_scales", tag="m_scales", align_bytes=64)
            mean_q[s] = (codes, scales)
            quantise(
                grouped[s][:].rearrange("p x g r t -> p (x g r t)"),
                codes[:].rearrange("p x g r -> p (x g r)"),
                scales[:].rearrange("p x g r -> p (x g r)"),
            )

        def transpose_words(rows, dst):
            bank = psum.tile([P, 4, P], F32, name="bank", tag="bank")
            for k in range(4):
                nc.tensor.transpose(out=bank[:, k, :], in_=rows[k], identity=ident[:])
            nc.scalar.copy(
                out=dst.bitcast(F32).rearrange("p g (r u) -> p g r u", u=2), in_=bank[:].rearrange("p (g u) r -> p g r u", u=2)
            )

        def load_feat(q):
            cols = slice(4 * q, 4 * q + 4)
            text = work.tile([P, 4, 256], BF16, name="text", tag="text")
            nc.sync.dma_start(out=text[:], in_=text_v[:, cols, :])
            imgf = work.tile([P, 4, 256], BF16, name="imgf", tag="imgf")
            nc.sync.dma_start(out=imgf[:], in_=imgf_v[:, cols, :])
            comp = work.tile([P, 4, 512], BF16, name="comp", tag="comp")
            nc.sync.dma_start(out=comp[:], in_=comp_v[:, cols, :])
            feats[q] = (text, imgf, comp)

        def transpose_feat(s):
            rho, ti = divmod(s, 2)
            if ti == 0:
                fg = work.tile([P, PASSES, 2, 4 * P], BF16, name="fg", tag="fg", align_bytes=64)
                grouped[("f", rho)] = fg
            q, i = divmod(s, 4)
            text, imgf, comp = feats[q]
            rows = [
                text[:, i, :].bitcast(F32),
                imgf[:, i, :].bitcast(F32),
                comp[:, i, 0:256].bitcast(F32),
                comp[:, i, 256:512].bitcast(F32),
            ]
            transpose_words(rows, grouped[("f", rho)][:, :, ti, :])

        def quantise_feat(rho):
            codes = work.tile([P, PASSES, 2 * P], U32, name="f_codes", tag="f_codes", align_bytes=64)
            scales = work.tile([P, PASSES, 2 * P], U8, name="f_scales", tag="f_scales", align_bytes=64)
            feat_q[rho] = (codes, scales)
            quantise(
                grouped[("f", rho)][:].rearrange("p g t w -> p (g t w)"),
                codes[:].rearrange("p g n -> p (g n)"),
                scales[:].rearrange("p g n -> p (g n)"),
            )

        def transpose_w_user():
            for j in range(CHUNKS):
                words = wu_raw[:, j, :].bitcast(F32)
                transpose_words([words[:, P * k : P * (k + 1)] for k in range(4)], wu_grouped[:, j, :, :])

        def quantise_w_user():
            for half in range(2):
                js = slice(4 * half, 4 * half + 4)
                quantise(
                    wu_grouped[:, js].rearrange("p j g w -> p (j g w)"),
                    wu_codes[:, js].rearrange("p j g r -> p (j g r)"),
                    wu_scales[:, js].rearrange("p j g r -> p (j g r)"),
                )

        def transpose_w_out(half):
            if half == 0:
                sg = keep.tile([P, 4, PASSES, 2, P, 4], BF16, name="sg", tag="wgroup", align_bytes=64)
                grouped["ws"] = sg
            sg = grouped["ws"]
            for m in (2 * half, 2 * half + 1):
                for a in range(2):
                    for g in range(PASSES):
                        bank = psum.tile([P, 4, P], BF16, name="bank_bf", tag="bank")
                        for t in range(4):
                            j = 4 * g + t
                            nc.tensor.transpose(out=bank[:, t, :], in_=ws_raw[:, m, a, P * j : P * (j + 1)], identity=ident_bf[:])
                        nc.scalar.copy(out=sg[:, m, g, a, :, :], in_=bank[:].rearrange("p t r -> p r t"))

        def quantise_w_out(half):
            ms = slice(2 * half, 2 * half + 2)
            quantise(
                grouped["ws"][:, ms].rearrange("p m g a r t -> p (m g a r t)"),
                ws_codes[:, ms].rearrange("p m g o -> p (m g o)"),
                ws_scales[:, ms].rearrange("p m g o -> p (m g o)"),
            )

        def stage1(rho):
            codes, scales = feat_q[rho]
            up = work.tile([P, CHUNKS, 2 * P], BF16, name="up", tag="up")
            planes[rho] = up
            for b in range(CHUNKS // 2):
                ub = psum.tile([P, 2, 2 * P], F32, name="ub", tag="bank")
                for jj in range(2):
                    j = 2 * b + jj
                    for g in range(PASSES):
                        nc.tensor.matmul_mx(
                            out=ub[:, jj, :],
                            lhsT=wu_codes[:, j, g, :].bitcast(FP8X4),
                            lhsT_scale=wu_scales[:, j, g, :],
                            rhs=codes[:, g, :].bitcast(FP8X4),
                            rhs_scale=scales[:, g, :],
                            start=(g == 0),
                            stop=(g == PASSES - 1),
                        )
                for jj in range(2):
                    j = 2 * b + jj
                    nc.scalar.activation(out=up[:, j, :], in_=ub[:, jj, :], func=ACT.Identity, bias=bu[:, j : j + 1])

        def regroup_u(rho):
            ug = work.tile([P, PASSES, 2 * P, 4], BF16, name="ug", tag="ug", align_bytes=64)
            grouped[("u", rho)] = ug
            for g in range(PASSES):
                nc.vector.tensor_copy(
                    out=ug[:, g, :, :].rearrange("p (c i) t -> p c t i", i=4),
                    in_=planes[rho][:, 4 * g : 4 * g + 4, :].rearrange("p t (c i) -> p c t i", i=4),
                )

        def quantise_u(rho):
            codes = work.tile([P, PASSES, 2 * P], U32, name="u_codes", tag="u_codes", align_bytes=64)
            scales = work.tile([P, PASSES, 2 * P], U8, name="u_scales", tag="u_scales", align_bytes=64)
            u_q[rho] = (codes, scales)
            quantise(
                grouped[("u", rho)][:].rearrange("p g n t -> p (g n t)"),
                codes[:].rearrange("p g n -> p (g n)"),
                scales[:].rearrange("p g n -> p (g n)"),
            )

        def stage2(rho):
            ob = psum.tile([P, 2, O], F32, name="ob", tag="bank")
            acc[rho] = ob
            u_codes, u_scales = u_q[rho]
            for ti in range(2):
                m_codes, m_scales = mean_q[2 * rho + ti]
                cols = slice(P * ti, P * (ti + 1))
                left = []
                for g in range(PASSES):
                    left.append((m_codes[:, 0, g, :], m_scales[:, 0, g, :], 0, g))
                    left.append((u_codes[:, g, cols], u_scales[:, g, cols], 1, g))
                    left.append((m_codes[:, 1, g, :], m_scales[:, 1, g, :], 2, g))
                    left.append((u_codes[:, g, cols], u_scales[:, g, cols], 3, g))
                for i, (codes, scales, m, g) in enumerate(left):
                    nc.tensor.matmul_mx(
                        out=ob[:, ti, :],
                        lhsT=codes.bitcast(FP8X4),
                        lhsT_scale=scales,
                        rhs=ws_codes[:, m, g, :].bitcast(FP8X4),
                        rhs_scale=ws_scales[:, m, g, :],
                        start=(i == 0),
                        stop=(i == len(left) - 1),
                    )

        def add_bias(rho):
            res = work.tile([P, 2, O], F32, name="res", tag="res")
            results[rho] = res
            nc.vector.tensor_tensor(out=res[:], in0=acc[rho][:], in1=bl2[:], op=ADD)

        def relu(rho):
            nc.vector.tensor_scalar_max(out=results[rho][:], in0=results[rho][:], scalar1=0.0)

        def store(rho):
            nc.sync.dma_start(out=out_v[:, 2 * rho : 2 * rho + 2, :], in_=results[rho][:])

        load_base(0)
        load_feat(0)
        for i in range(4):
            nc.sync.dma_start(out=wu_raw[:, 2 * i : 2 * i + 2, :], in_=wu_v[:, 2 * i : 2 * i + 2, :])
        load_base(1)
        load_base(2)
        for m, w in enumerate((Wl_img, Wr_img, Wl_txt, Wr_txt)):
            nc.sync.dma_start(out=ws_raw[:, m], in_=w.rearrange("(a p) h -> p a h", a=2))
        load_base(3)

        def tile_at(s):
            return 0 <= s < TILES

        def round_at(twice):
            return twice // 2 if twice % 2 == 0 and 0 <= twice // 2 < ROUNDS else None

        for s in range(-1, TILES + 8):
            if round_at(s - 7) is not None:
                store(round_at(s - 7))
            if tile_at(s):
                add_nodes(s)
            if round_at(s - 6) is not None:
                add_bias(round_at(s - 6))
            if s == 0:
                bu_t = psum.tile([P, P], BF16, name="bu_t", tag="bank")
                nc.tensor.transpose(out=bu_t[:], in_=bu_rows[:], identity=ident_bf[:])
                nc.vector.tensor_copy(out=bu[:], in_=bu_t[:, 0:CHUNKS])
                for ti in range(2):
                    nc.vector.tensor_tensor(out=bl2[:, ti, :], in0=bl_a[:], in1=bl_b[:], op=ADD)
            if tile_at(s - 1):
                transpose_means(s - 1)
                if s - 1 + BASE_BUFS < TILES:
                    load_base(s - 1 + BASE_BUFS)
            if tile_at(s + 1):
                transpose_feat(s + 1)
            if s % 4 == 0 and 1 <= s // 4 + 1 < TILES // 4:
                load_feat(s // 4 + 1)
            if s == 0:
                transpose_w_user()
            if s in (2, 3):
                transpose_w_out(s - 2)
            if round_at(s - 5) is not None:
                stage2(round_at(s - 5))
            if round_at(s - 2) is not None:
                stage1(round_at(s - 2))
            if tile_at(s - 2):
                quantise_means(s - 2)
            if round_at(s - 1) is not None:
                quantise_feat(round_at(s - 1))
            if s == 1:
                quantise_w_user()
            if s in (3, 4):
                quantise_w_out(s - 3)
            if round_at(s - 3) is not None:
                regroup_u(round_at(s - 3))
            if round_at(s - 4) is not None:
                quantise_u(round_at(s - 4))
            if round_at(s - 6) is not None:
                relu(round_at(s - 6))
